import numpy as np
import ml_dtypes


def mxq(x, axis, fmt="e4m3"):
    dtype, down = {"e4m3": (ml_dtypes.float8_e4m3fn, 7), "e5m2": (ml_dtypes.float8_e5m2, 14)}[fmt]
    v = np.moveaxis(np.asarray(x, np.float32).astype(ml_dtypes.bfloat16).astype(np.float64), axis, -1)
    blocks = v.reshape(v.shape[:-1] + (-1, 32))
    amax = np.abs(blocks).max(-1, keepdims=True)
    byte = np.maximum(np.where(amax > 0, np.frexp(amax)[1] - 1 + 127, 0) - down, 1)
    scale = np.exp2(byte - 127.0)
    codes = (blocks / scale).astype(np.float32).astype(dtype).astype(np.float64)
    return np.moveaxis((codes * scale).reshape(v.shape), -1, axis)


WIDE = False


def mx_kscale(k):
    if not WIDE:
        return np.ones(k)
    levels = np.array([10, -10, 5, -5, 0])
    a = np.random.permutation(np.resize(levels, k // 512 * 4)).reshape(k // 512, 4)
    idx = np.arange(k)
    return np.exp2(a[idx // 512, idx % 128 // 32])


BF16 = ml_dtypes.bfloat16


def bf(x):
    return np.asarray(x, np.float32).astype(BF16)


def f64(x):
    return np.asarray(x).astype(np.float64)


E2M1 = np.array([0.0, 0.5, 1.0, 1.5, 2.0, 3.0, 4.0, 6.0, -0.0, -0.5, -1.0, -1.5, -2.0, -3.0, -4.0, -6.0])


def pack_weight(w, fmt):
    k, n = w.shape
    w = f64(bf(w)).reshape(k // 32, 32, n)
    amax = np.abs(w).max(1)
    if fmt == "e4m3":
        byte = np.frexp(amax)[1] - 1 + 127 - 7
    else:
        mant, ex = np.frexp(amax / 6.0)
        byte = np.where(mant > 0.5, ex, ex - 1) + 127
    byte = np.clip(np.where(amax > 0, byte, 1), 1, 254)
    scaled = (w * np.exp2(127.0 - byte)[:, None, :]).reshape(k, n).astype(np.float32)
    by_word = np.ascontiguousarray(scaled.reshape(k // 512, 128, 4, n).transpose(0, 1, 3, 2))
    if fmt == "e4m3":
        words = by_word.astype(ml_dtypes.float8_e4m3fn).view(np.uint8)
    else:
        c = by_word.astype(ml_dtypes.float4_e2m1fn).view(np.uint8) & 0xF
        words = c[..., 0::2] | (c[..., 1::2] << 4)
    return np.ascontiguousarray(words), np.ascontiguousarray(byte.astype(np.uint8).reshape(k // 512, 16, n))


def unpack_weight(words, scales, fmt):
    g, p, n, _ = words.shape
    if fmt == "e4m3":
        vals = np.ascontiguousarray(words).view(ml_dtypes.float8_e4m3fn).astype(np.float64)
    else:
        nib = np.empty((g, p, n, 4), np.uint8)
        nib[..., 0::2] = words & 0xF
        nib[..., 1::2] = words >> 4
        vals = E2M1[nib]
    vals = vals * np.repeat(np.exp2(scales.astype(np.float64) - 127.0), 8, axis=1)[..., None]
    return vals.transpose(0, 1, 3, 2).reshape(g * 512, n)


B, IN, H = 128, 8192, 512
FMT = "e4m3"


def hard_sigmoid(v):
    return np.clip(v / 6.0 + 0.5, 0.0, 1.0)


def hard_tanh(v):
    return np.clip(v, -1.0, 1.0)


def setup_inputs():
    s, t = mx_kscale(IN), mx_kscale(H)
    input_ = bf(np.random.standard_normal((B, IN)) * s)
    h_0 = bf(np.random.standard_normal((B, H)) * t)
    c_0 = bf(np.random.standard_normal((B, H)))
    W_ih = np.random.standard_normal((4 * H, IN)) * 1.25 / np.sqrt(IN) / s[None, :]
    W_hh = np.random.standard_normal((4 * H, H)) * 1.25 / np.sqrt(H) / t[None, :]
    b_hh = bf(np.random.standard_normal(4 * H) * 0.3)
    W_ih_words, W_ih_scales = pack_weight(np.ascontiguousarray(W_ih.T), FMT)
    W_hh_words, W_hh_scales = pack_weight(np.ascontiguousarray(W_hh.T), FMT)
    return {"input_": input_,
            "h_0": h_0,
            "c_0": c_0,
            "W_ih_words": W_ih_words,
            "W_ih_scales": W_ih_scales,
            "W_hh_words": W_hh_words,
            "W_hh_scales": W_hh_scales,
            "b_hh": b_hh}


def reference(input_, h_0, c_0, W_ih_words, W_ih_scales, W_hh_words, W_hh_scales, b_hh):
    wi = mxq(f64(input_), 1, "e4m3") @ unpack_weight(W_ih_words, W_ih_scales, FMT)
    wh_b = (mxq(f64(h_0), 1, "e4m3") @ unpack_weight(W_hh_words, W_hh_scales, FMT)) + f64(b_hh)
    h_x4 = wh_b + wi
    f, i, o, g = np.split(h_x4, 4, axis=1)
    new = hard_sigmoid(i) * hard_tanh(g)
    old = hard_sigmoid(f) * f64(c_0)
    c_1 = old + new
    h_1 = hard_sigmoid(o) * hard_tanh(c_1)
    return (h_1, c_1)

@@ -1,0 +1,192 @@
+from contextlib import ExitStack
+
+import concourse.masks as masks
+import concourse.mybir as mybir
+
+F32 = mybir.dt.float32
+BF16 = mybir.dt.bfloat16
+I32 = mybir.dt.int32
+U32 = mybir.dt.uint32
+U8 = mybir.dt.uint8
+FP8X4 = mybir.dt.float8_e4m3fn_x4
+ALU = mybir.AluOpType
+
+P = 128
+PACK = 4
+K_PASS = P * PACK
+IN = 8192
+H = 512
+IH_PASSES = IN // K_PASS
+PASSES = 1 + IH_PASSES
+QUADRANTS = 4
+ROWS = 4
+PLANES = 4
+
+GATE_F, GATE_I, GATE_O, GATE_G = 0, 1, 2, 3
+HARD_SIGMOID = (1.0 / 6.0, 0.5, 0.0, 1.0)
+HARD_TANH = (1.0, 0.0, -1.0, 1.0)
+GATE_FUNCTION = {GATE_F: HARD_SIGMOID, GATE_I: HARD_SIGMOID, GATE_O: HARD_SIGMOID, GATE_G: HARD_TANH}
+
+TAIL_PASSES = 4
+WHOLE_PIECE = (GATE_F, GATE_I, GATE_O, GATE_G)
+TAIL_PIECES = ((GATE_F, GATE_I), (GATE_G,), (GATE_O,))
+
+FLOPS = 2 * P * (IN + H) * 4 * H
+
+
+def weight_stream():
+    first_tail_pass = PASSES - TAIL_PASSES
+    stream = [(s, WHOLE_PIECE) for s in range(first_tail_pass)]
+    for piece in TAIL_PIECES:
+        stream.extend([(s, piece) for s in range(first_tail_pass, PASSES)])
+    return stream
+
+
+def tile_qlstmcell_k_kernel(
+    tc, input_, h_0, c_0, W_ih_words, W_ih_scales, W_hh_words, W_hh_scales, b_hh, out_0, out_1
+):
+    nc = tc.nc
+    with ExitStack() as ctx:
+        keep = ctx.enter_context(tc.tile_pool(name="keep", bufs=1))
+        stage = ctx.enter_context(tc.tile_pool(name="stage", bufs=3))
+        acc_pool = ctx.enter_context(tc.psum_pool(name="acc", bufs=1))
+        work_pool = ctx.enter_context(tc.psum_pool(name="work", bufs=4))
+        ctx.enter_context(tc.manual_schedule())
+
+        hh_planes = keep.tile([P, H], U8, align_bytes=64)
+        nc.vector.memset(hh_planes[:].bitcast(I32), 0)
+        ih_planes = []
+        for tile_no in range(IH_PASSES // PLANES):
+            planes = keep.tile([P, 4 * H], U8, align_bytes=64, name="ih_planes%d" % tile_no)
+            nc.vector.memset(planes[:].bitcast(I32), 0)
+            ih_planes.append(planes)
+
+        identity = keep.tile([P, P], F32)
+        masks.make_identity(nc, identity[:])
+        bias_rows = keep.tile([P, 4 * H], BF16)
+        nc.gpsimd.memset(bias_rows[:], 0.0)
+        ones = keep.tile([P, P], BF16)
+        nc.gpsimd.memset(ones[:], 1.0)
+
+        h_sb = keep.tile([P, H], BF16)
+        nc.sync.dma_start(out=h_sb[:], in_=h_0)
+        x_sb = keep.tile([P, IN], BF16)
+        nc.sync.dma_start(out=x_sb[:], in_=input_)
+        c_sb = keep.tile([P, H], BF16)
+        nc.scalar.dma_start(out=c_sb[:], in_=c_0)
+        nc.scalar.dma_start(out=bias_rows[0:1, :], in_=b_hh.unsqueeze(0))
+
+        for quadrant in range(QUADRANTS):
+            rows = slice(ROWS * quadrant, ROWS * (quadrant + 1))
+            nc.sync.dma_start(
+                out=hh_planes[32 * quadrant : 32 * quadrant + 16, :].bitcast(I32),
+                in_=W_hh_scales[0, rows, :].rearrange("r (j n) -> j r n", j=PLANES).bitcast(I32),
+            )
+        for tile_no in range(IH_PASSES // PLANES):
+            for quadrant in range(QUADRANTS):
+                rows = slice(ROWS * quadrant, ROWS * (quadrant + 1))
+                nc.sync.dma_start(
+                    out=ih_planes[tile_no][32 * quadrant : 32 * quadrant + 16, :].bitcast(I32),
+                    in_=W_ih_scales[PLANES * tile_no : PLANES * (tile_no + 1), rows, :].bitcast(I32),
+                )
+
+        stream = weight_stream()
+        word_tiles = []
+        for s, piece in stream:
+            words = W_hh_words[0] if s == 0 else W_ih_words[s - 1]
+            first_byte = PACK * H * piece[0]
+            n_bytes = PACK * H * len(piece)
+            tile = keep.tile([P, H * len(piece)], U32, align_bytes=64, name="w%d_%d" % (s, piece[0]))
+            nc.sync.dma_start(
+                out=tile[:].bitcast(I32),
+                in_=words.rearrange("p n t -> p (n t)")[:, first_byte : first_byte + n_bytes].bitcast(I32),
+            )
+            word_tiles.append(tile)
+
+        x_codes = keep.tile([P, PASSES, P], U32, align_bytes=64)
+        x_scales = keep.tile([P, PASSES, P], U8, align_bytes=64)
+
+        def quantise_passes(words, first_pass, n_passes, copy_out):
+            flipped = work_pool.tile([P, n_passes, 2, P], F32, tag="work")
+            for s in range(n_passes):
+                for u in range(2):
+                    nc.tensor.transpose(
+                        flipped[:, s, u, :], words[:, 256 * s + u : 256 * (s + 1) : 2], identity[:]
+                    )
+            grouped = stage.tile([P, n_passes, P, PACK], BF16, align_bytes=64, tag="grouped")
+            copy_out(out=grouped[:].bitcast(F32), in_=flipped[:].rearrange("p s u b -> p s b u"))
+            passes = slice(first_pass, first_pass + n_passes)
+            nc.vector.quantize_mx(
+                out=x_codes[:, passes, :].rearrange("p s b -> p (s b)").bitcast(FP8X4),
+                scales=x_scales[:, passes, :].rearrange("p s b -> p (s b)"),
+                in_=grouped[:].rearrange("p s b t -> p (s b t)"),
+            )
+
+        quantise_passes(h_sb[:].bitcast(F32), 0, 1, nc.vector.tensor_copy)
+        x_words = x_sb[:].bitcast(F32)
+        for pair in range(IH_PASSES // 2):
+            quantise_passes(
+                x_words[:, 512 * pair : 512 * (pair + 1)],
+                1 + 2 * pair,
+                2,
+                nc.scalar.copy if pair % 2 == 0 else nc.vector.tensor_copy,
+            )
+
+        gate_bias = keep.tile([P, 4, H], F32)
+        for gate in range(4):
+            scale, shift = GATE_FUNCTION[gate][:2]
+            spread = work_pool.tile([P, H], F32, tag="work")
+            nc.tensor.matmul(
+                out=spread[:], lhsT=ones[:], rhs=bias_rows[:, H * gate : H * (gate + 1)], start=True, stop=True
+            )
+            nc.vector.tensor_scalar(
+                out=gate_bias[:, gate, :], in0=spread[:], scalar1=scale, scalar2=shift, op0=ALU.mult, op1=ALU.add
+            )
+
+        sums = [acc_pool.tile([P, H], F32, name="sums%d" % gate) for gate in range(4)]
+        for (s, piece), tile in zip(stream, word_tiles):
+            for place, gate in enumerate(piece):
+                if s == 0:
+                    plane = hh_planes[ROWS * gate : P, :]
+                else:
+                    group = s - 1
+                    plane = ih_planes[group // PLANES][ROWS * (group % PLANES) : P, H * gate : H * (gate + 1)]
+                nc.tensor.matmul_mx(
+                    out=sums[gate][:],
+                    lhsT=x_codes[:, s, :].bitcast(FP8X4),
+                    lhsT_scale=x_scales[:, s, :],
+                    rhs=tile[:, H * place : H * (place + 1)].bitcast(FP8X4),
+                    rhs_scale=plane,
+                    start=(s == 0),
+                    stop=(s == PASSES - 1),
+                )
+
+        def gate_value(gate):
+            scale, shift, low, high = GATE_FUNCTION[gate]
+            value = keep.tile([P, H], F32, name="gate%d" % gate)
+            nc.vector.scalar_tensor_tensor(
+                out=value[:], in0=sums[gate][:], scalar=scale, in1=gate_bias[:, gate, :], op0=ALU.mult, op1=ALU.add
+            )
+            nc.vector.tensor_scalar(
+                out=value[:], in0=value[:], scalar1=low, scalar2=high, op0=ALU.max, op1=ALU.min
+            )
+            return value
+
+        forget = gate_value(GATE_F)
+        old = keep.tile([P, H], F32)
+        nc.vector.tensor_tensor(out=old[:], in0=forget[:], in1=c_sb[:], op=ALU.mult)
+        take_in = gate_value(GATE_I)
+        candidate = gate_value(GATE_G)
+        new = keep.tile([P, H], F32)
+        nc.vector.tensor_tensor(out=new[:], in0=take_in[:], in1=candidate[:], op=ALU.mult)
+        c_1 = keep.tile([P, H], F32)
+        nc.vector.tensor_tensor(out=c_1[:], in0=old[:], in1=new[:], op=ALU.add)
+        nc.sync.dma_start(out=out_1, in_=c_1[:])
+        c_clipped = keep.tile([P, H], F32)
+        nc.vector.tensor_scalar(
+            out=c_clipped[:], in0=c_1[:], scalar1=-1.0, scalar2=1.0, op0=ALU.max, op1=ALU.min
+        )
+        let_out = gate_value(GATE_O)
+        h_1 = keep.tile([P, H], F32)
+        nc.vector.tensor_tensor(out=h_1[:], in0=let_out[:], in1=c_clipped[:], op=ALU.mult)
+        nc.sync.dma_start(out=out_0, in_=h_1[:])

@@ -64,9 +64,9 @@ def tile_qlstmcell_k_kernel(
         identity = keep.tile([P, P], F32)
         masks.make_identity(nc, identity[:])
         bias_rows = keep.tile([P, 4 * H], BF16)
-        nc.gpsimd.memset(bias_rows[:], 0.0)
+        nc.vector.memset(bias_rows[:].bitcast(I32), 0)
         ones = keep.tile([P, P], BF16)
-        nc.gpsimd.memset(ones[:], 1.0)
+        nc.vector.memset(ones[:], 1.0)
 
         h_sb = keep.tile([P, H], BF16)
         nc.sync.dma_start(out=h_sb[:], in_=h_0)
@@ -78,16 +78,16 @@ def tile_qlstmcell_k_kernel(
 
         for quadrant in range(QUADRANTS):
             rows = slice(ROWS * quadrant, ROWS * (quadrant + 1))
-            nc.sync.dma_start(
-                out=hh_planes[32 * quadrant : 32 * quadrant + 16, :].bitcast(I32),
-                in_=W_hh_scales[0, rows, :].rearrange("r (j n) -> j r n", j=PLANES).bitcast(I32),
+            nc.gpsimd.dma_start(
+                out=hh_planes[32 * quadrant : 32 * quadrant + 16, :].bitcast(F32),
+                in_=W_hh_scales[0, rows, :].rearrange("r (j n) -> j r n", j=PLANES).bitcast(F32),
             )
         for tile_no in range(IH_PASSES // PLANES):
             for quadrant in range(QUADRANTS):
                 rows = slice(ROWS * quadrant, ROWS * (quadrant + 1))
-                nc.sync.dma_start(
-                    out=ih_planes[tile_no][32 * quadrant : 32 * quadrant + 16, :].bitcast(I32),
-                    in_=W_ih_scales[PLANES * tile_no : PLANES * (tile_no + 1), rows, :].bitcast(I32),
+                nc.gpsimd.dma_start(
+                    out=ih_planes[tile_no][32 * quadrant : 32 * quadrant + 16, :].bitcast(F32),
+                    in_=W_ih_scales[PLANES * tile_no : PLANES * (tile_no + 1), rows, :].bitcast(F32),
                 )
 
         stream = weight_stream()

@@ -27,9 +27,11 @@ HARD_SIGMOID = (1.0 / 6.0, 0.5, 0.0, 1.0)
 HARD_TANH = (1.0, 0.0, -1.0, 1.0)
 GATE_FUNCTION = {GATE_F: HARD_SIGMOID, GATE_I: HARD_SIGMOID, GATE_O: HARD_SIGMOID, GATE_G: HARD_TANH}
 
-TAIL_PASSES = 4
+TAIL_PASSES = 5
 WHOLE_PIECE = (GATE_F, GATE_I, GATE_O, GATE_G)
 TAIL_PIECES = ((GATE_F, GATE_I), (GATE_G,), (GATE_O,))
+
+HALVES = (slice(0, H // 2), slice(H // 2, H))
 
 FLOPS = 2 * P * (IN + H) * 4 * H
 
@@ -161,32 +163,50 @@ def tile_qlstmcell_k_kernel(
                     stop=(s == PASSES - 1),
                 )
 
-        def gate_value(gate):
-            scale, shift, low, high = GATE_FUNCTION[gate]
-            value = keep.tile([P, H], F32, name="gate%d" % gate)
-            nc.vector.scalar_tensor_tensor(
-                out=value[:], in0=sums[gate][:], scalar=scale, in1=gate_bias[:, gate, :], op0=ALU.mult, op1=ALU.add
-            )
-            nc.vector.tensor_scalar(
-                out=value[:], in0=value[:], scalar1=low, scalar2=high, op0=ALU.max, op1=ALU.min
-            )
-            return value
+        def gate_values(gates):
+            values = {}
+            for gate in gates:
+                scale = GATE_FUNCTION[gate][0]
+                values[gate] = keep.tile([P, H], F32, name="gate%d" % gate)
+                for cols in HALVES:
+                    nc.vector.scalar_tensor_tensor(
+                        out=values[gate][:, cols],
+                        in0=sums[gate][:, cols],
+                        scalar=scale,
+                        in1=gate_bias[:, gate, cols],
+                        op0=ALU.mult,
+                        op1=ALU.add,
+                    )
+            for gate in gates:
+                low, high = GATE_FUNCTION[gate][2:]
+                clip(values[gate], values[gate], low, high)
+            return values
 
-        forget = gate_value(GATE_F)
+        def clip(out, in0, low, high):
+            for cols in HALVES:
+                nc.vector.tensor_scalar(
+                    out=out[:, cols], in0=in0[:, cols], scalar1=low, scalar2=high, op0=ALU.max, op1=ALU.min
+                )
+
+        def combine(out, in0, in1, op):
+            for cols in HALVES:
+                nc.vector.tensor_tensor(out=out[:, cols], in0=in0[:, cols], in1=in1[:, cols], op=op)
+
+        first = gate_values((GATE_F, GATE_I))
         old = keep.tile([P, H], F32)
-        nc.vector.tensor_tensor(out=old[:], in0=forget[:], in1=c_sb[:], op=ALU.mult)
-        take_in = gate_value(GATE_I)
-        candidate = gate_value(GATE_G)
+        combine(old, first[GATE_F], c_sb, ALU.mult)
+
+        candidate = gate_values((GATE_G,))[GATE_G]
         new = keep.tile([P, H], F32)
-        nc.vector.tensor_tensor(out=new[:], in0=take_in[:], in1=candidate[:], op=ALU.mult)
+        combine(new, first[GATE_I], candidate, ALU.mult)
         c_1 = keep.tile([P, H], F32)
-        nc.vector.tensor_tensor(out=c_1[:], in0=old[:], in1=new[:], op=ALU.add)
+        combine(c_1, old, new, ALU.add)
         nc.sync.dma_start(out=out_1, in_=c_1[:])
         c_clipped = keep.tile([P, H], F32)
-        nc.vector.tensor_scalar(
-            out=c_clipped[:], in0=c_1[:], scalar1=-1.0, scalar2=1.0, op0=ALU.max, op1=ALU.min
-        )
-        let_out = gate_value(GATE_O)
+        clip(c_clipped, c_1, -1.0, 1.0)
+
+        let_out = gate_values((GATE_O,))[GATE_O]
         h_1 = keep.tile([P, H], F32)
-        nc.vector.tensor_tensor(out=h_1[:], in0=let_out[:], in1=c_clipped[:], op=ALU.mult)
-        nc.sync.dma_start(out=out_0, in_=h_1[:])
+        combine(h_1, let_out, c_clipped, ALU.mult)
+        for cols in HALVES:
+            nc.sync.dma_start(out=out_0[:, cols], in_=h_1[:, cols])

@@ -28,20 +28,32 @@ HARD_TANH = (1.0, 0.0, -1.0, 1.0)
 GATE_FUNCTION = {GATE_F: HARD_SIGMOID, GATE_I: HARD_SIGMOID, GATE_O: HARD_SIGMOID, GATE_G: HARD_TANH}
 
 TAIL_PASSES = 5
-WHOLE_PIECE = (GATE_F, GATE_I, GATE_O, GATE_G)
-TAIL_PIECES = ((GATE_F, GATE_I), (GATE_G,), (GATE_O,))
+SPLIT_PASSES = 3
 
+F_BLOCK = (GATE_F, 0, H)
+I_BLOCK = (GATE_I, 0, H)
+G_BLOCK = (GATE_G, 0, H)
+O_LEFT = (GATE_O, 0, H // 2)
+O_RIGHT = (GATE_O, H // 2, H // 2)
+BLOCKS = (F_BLOCK, I_BLOCK, O_LEFT, O_RIGHT, G_BLOCK)
 HALVES = (slice(0, H // 2), slice(H // 2, H))
 
 FLOPS = 2 * P * (IN + H) * 4 * H
 
 
 def weight_stream():
-    first_tail_pass = PASSES - TAIL_PASSES
-    stream = [(s, WHOLE_PIECE) for s in range(first_tail_pass)]
-    for piece in TAIL_PIECES:
-        stream.extend([(s, piece) for s in range(first_tail_pass, PASSES)])
+    tail = range(PASSES - TAIL_PASSES, PASSES)
+    stream = [(s, BLOCKS) for s in range(PASSES - TAIL_PASSES)]
+    stream.extend([(s, (F_BLOCK, I_BLOCK)) for s in tail])
+    stream.extend([(s, (G_BLOCK,)) for s in tail])
+    stream.extend([(s, (O_LEFT, O_RIGHT)) for s in tail[:-SPLIT_PASSES]])
+    stream.extend([(s, (O_LEFT,)) for s in tail[-SPLIT_PASSES:]])
+    stream.extend([(s, (O_RIGHT,)) for s in tail[-SPLIT_PASSES:]])
     return stream
+
+
+def first_column(block):
+    return H * block[0] + block[1]
 
 
 def tile_qlstmcell_k_kernel(
@@ -52,7 +64,7 @@ def tile_qlstmcell_k_kernel(
         keep = ctx.enter_context(tc.tile_pool(name="keep", bufs=1))
         stage = ctx.enter_context(tc.tile_pool(name="stage", bufs=3))
         acc_pool = ctx.enter_context(tc.psum_pool(name="acc", bufs=1))
-        work_pool = ctx.enter_context(tc.psum_pool(name="work", bufs=4))
+        work_pool = ctx.enter_context(tc.psum_pool(name="work", bufs=3))
         ctx.enter_context(tc.manual_schedule())
 
         hh_planes = keep.tile([P, H], U8, align_bytes=64)
@@ -96,9 +108,10 @@ def tile_qlstmcell_k_kernel(
         word_tiles = []
         for s, piece in stream:
             words = W_hh_words[0] if s == 0 else W_ih_words[s - 1]
-            first_byte = PACK * H * piece[0]
-            n_bytes = PACK * H * len(piece)
-            tile = keep.tile([P, H * len(piece)], U32, align_bytes=64, name="w%d_%d" % (s, piece[0]))
+            width = sum([block[2] for block in piece])
+            first_byte = PACK * first_column(piece[0])
+            n_bytes = PACK * width
+            tile = keep.tile([P, width], U32, align_bytes=64, name="w%d_%d" % (s, first_column(piece[0])))
             nc.sync.dma_start(
                 out=tile[:].bitcast(I32),
                 in_=words.rearrange("p n t -> p (n t)")[:, first_byte : first_byte + n_bytes].bitcast(I32),
@@ -145,68 +158,75 @@ def tile_qlstmcell_k_kernel(
                 out=gate_bias[:, gate, :], in0=spread[:], scalar1=scale, scalar2=shift, op0=ALU.mult, op1=ALU.add
             )
 
-        sums = [acc_pool.tile([P, H], F32, name="sums%d" % gate) for gate in range(4)]
+        sums = {block: acc_pool.tile([P, block[2]], F32, name="sums%d" % first_column(block)) for block in BLOCKS}
         for (s, piece), tile in zip(stream, word_tiles):
-            for place, gate in enumerate(piece):
+            for block in piece:
+                gate, start, width = block
+                place = first_column(block) - first_column(piece[0])
                 if s == 0:
-                    plane = hh_planes[ROWS * gate : P, :]
+                    plane = hh_planes[ROWS * gate : P, start : start + width]
                 else:
                     group = s - 1
-                    plane = ih_planes[group // PLANES][ROWS * (group % PLANES) : P, H * gate : H * (gate + 1)]
+                    column = first_column(block)
+                    plane = ih_planes[group // PLANES][ROWS * (group % PLANES) : P, column : column + width]
                 nc.tensor.matmul_mx(
-                    out=sums[gate][:],
+                    out=sums[block][:],
                     lhsT=x_codes[:, s, :].bitcast(FP8X4),
                     lhsT_scale=x_scales[:, s, :],
-                    rhs=tile[:, H * place : H * (place + 1)].bitcast(FP8X4),
+                    rhs=tile[:, place : place + width].bitcast(FP8X4),
                     rhs_scale=plane,
                     start=(s == 0),
                     stop=(s == PASSES - 1),
                 )
 
-        def gate_values(gates):
-            values = {}
-            for gate in gates:
-                scale = GATE_FUNCTION[gate][0]
-                values[gate] = keep.tile([P, H], F32, name="gate%d" % gate)
-                for cols in HALVES:
+        values = [keep.tile([P, H], F32, name="gate%d" % gate) for gate in range(4)]
+
+        def halves(first, width):
+            return (slice(first, first + width // 2), slice(first + width // 2, first + width))
+
+        def gate_values(blocks):
+            for block in blocks:
+                gate, start, width = block
+                for cols in halves(0, width):
+                    in_gate = slice(start + cols.start, start + cols.stop)
                     nc.vector.scalar_tensor_tensor(
-                        out=values[gate][:, cols],
-                        in0=sums[gate][:, cols],
-                        scalar=scale,
-                        in1=gate_bias[:, gate, cols],
+                        out=values[gate][:, in_gate],
+                        in0=sums[block][:, cols],
+                        scalar=GATE_FUNCTION[gate][0],
+                        in1=gate_bias[:, gate, in_gate],
                         op0=ALU.mult,
                         op1=ALU.add,
                     )
-            for gate in gates:
+            for gate, start, width in blocks:
                 low, high = GATE_FUNCTION[gate][2:]
-                clip(values[gate], values[gate], low, high)
-            return values
+                clip(values[gate], values[gate], low, high, halves(start, width))
 
-        def clip(out, in0, low, high):
-            for cols in HALVES:
+        def clip(out, in0, low, high, parts=HALVES):
+            for cols in parts:
                 nc.vector.tensor_scalar(
                     out=out[:, cols], in0=in0[:, cols], scalar1=low, scalar2=high, op0=ALU.max, op1=ALU.min
                 )
 
-        def combine(out, in0, in1, op):
-            for cols in HALVES:
+        def combine(out, in0, in1, op, parts=HALVES):
+            for cols in parts:
                 nc.vector.tensor_tensor(out=out[:, cols], in0=in0[:, cols], in1=in1[:, cols], op=op)
 
-        first = gate_values((GATE_F, GATE_I))
+        gate_values((F_BLOCK, I_BLOCK))
         old = keep.tile([P, H], F32)
-        combine(old, first[GATE_F], c_sb, ALU.mult)
+        combine(old, values[GATE_F], c_sb, ALU.mult)
 
-        candidate = gate_values((GATE_G,))[GATE_G]
+        gate_values((G_BLOCK,))
         new = keep.tile([P, H], F32)
-        combine(new, first[GATE_I], candidate, ALU.mult)
+        combine(new, values[GATE_I], values[GATE_G], ALU.mult)
         c_1 = keep.tile([P, H], F32)
         combine(c_1, old, new, ALU.add)
         nc.sync.dma_start(out=out_1, in_=c_1[:])
         c_clipped = keep.tile([P, H], F32)
         clip(c_clipped, c_1, -1.0, 1.0)
 
-        let_out = gate_values((GATE_O,))[GATE_O]
         h_1 = keep.tile([P, H], F32)
-        combine(h_1, let_out, c_clipped, ALU.mult)
-        for cols in HALVES:
-            nc.sync.dma_start(out=out_0[:, cols], in_=h_1[:, cols])
+        for block in (O_LEFT, O_RIGHT):
+            start, width = block[1:]
+            gate_values((block,))
+            combine(h_1, values[GATE_O], c_clipped, ALU.mult, halves(start, width))
+            nc.sync.dma_start(out=out_0[:, start : start + width], in_=h_1[:, start : start + width])

@@ -27,7 +27,7 @@ HARD_SIGMOID = (1.0 / 6.0, 0.5, 0.0, 1.0)
 HARD_TANH = (1.0, 0.0, -1.0, 1.0)
 GATE_FUNCTION = {GATE_F: HARD_SIGMOID, GATE_I: HARD_SIGMOID, GATE_O: HARD_SIGMOID, GATE_G: HARD_TANH}
 
-TAIL_PASSES = 5
+TAIL_PASSES = 7
 SPLIT_PASSES = 3
 
 F_BLOCK = (GATE_F, 0, H)

@@ -82,11 +82,11 @@ def tile_qlstmcell_k_kernel(
         ones = keep.tile([P, P], BF16)
         nc.vector.memset(ones[:], 1.0)
 
-        h_sb = keep.tile([P, H], BF16)
+        h_sb = keep.tile([P, H], BF16, align_bytes=256)
         nc.sync.dma_start(out=h_sb[:], in_=h_0)
-        x_sb = keep.tile([P, IN], BF16)
+        x_sb = keep.tile([P, IN], BF16, align_bytes=256)
         nc.sync.dma_start(out=x_sb[:], in_=input_)
-        c_sb = keep.tile([P, H], BF16)
+        c_sb = keep.tile([P, H], BF16, align_bytes=256)
         nc.scalar.dma_start(out=c_sb[:], in_=c_0)
         nc.scalar.dma_start(out=bias_rows[0:1, :], in_=b_hh.unsqueeze(0))
 
@@ -111,7 +111,7 @@ def tile_qlstmcell_k_kernel(
             width = sum([block[2] for block in piece])
             first_byte = PACK * first_column(piece[0])
             n_bytes = PACK * width
-            tile = keep.tile([P, width], U32, align_bytes=64, name="w%d_%d" % (s, first_column(piece[0])))
+            tile = keep.tile([P, width], U32, align_bytes=256, name="w%d_%d" % (s, first_column(piece[0])))
             nc.sync.dma_start(
                 out=tile[:].bitcast(I32),
                 in_=words.rearrange("p n t -> p (n t)")[:, first_byte : first_byte + n_bytes].bitcast(I32),
@@ -218,13 +218,13 @@ def tile_qlstmcell_k_kernel(
         gate_values((G_BLOCK,))
         new = keep.tile([P, H], F32)
         combine(new, values[GATE_I], values[GATE_G], ALU.mult)
-        c_1 = keep.tile([P, H], F32)
+        c_1 = keep.tile([P, H], F32, align_bytes=256)
         combine(c_1, old, new, ALU.add)
         nc.sync.dma_start(out=out_1, in_=c_1[:])
         c_clipped = keep.tile([P, H], F32)
         clip(c_clipped, c_1, -1.0, 1.0)
 
-        h_1 = keep.tile([P, H], F32)
+        h_1 = keep.tile([P, H], F32, align_bytes=256)
         for block in (O_LEFT, O_RIGHT):
             start, width = block[1:]
             gate_values((block,))

@@ -67,26 +67,26 @@ def tile_qlstmcell_k_kernel(
         work_pool = ctx.enter_context(tc.psum_pool(name="work", bufs=3))
         ctx.enter_context(tc.manual_schedule())
 
-        hh_planes = keep.tile([P, H], U8, align_bytes=64)
+        hh_planes = keep.tile([P, H], U8, align_bytes=512)
         nc.vector.memset(hh_planes[:].bitcast(I32), 0)
         ih_planes = []
         for tile_no in range(IH_PASSES // PLANES):
-            planes = keep.tile([P, 4 * H], U8, align_bytes=64, name="ih_planes%d" % tile_no)
+            planes = keep.tile([P, 4 * H], U8, align_bytes=512, name="ih_planes%d" % tile_no)
             nc.vector.memset(planes[:].bitcast(I32), 0)
             ih_planes.append(planes)
 
         identity = keep.tile([P, P], F32)
         masks.make_identity(nc, identity[:])
-        bias_rows = keep.tile([P, 4 * H], BF16)
+        bias_rows = keep.tile([P, 4 * H], BF16, align_bytes=512)
         nc.vector.memset(bias_rows[:].bitcast(I32), 0)
         ones = keep.tile([P, P], BF16)
         nc.vector.memset(ones[:], 1.0)
 
-        h_sb = keep.tile([P, H], BF16, align_bytes=256)
+        h_sb = keep.tile([P, H], BF16, align_bytes=512)
         nc.sync.dma_start(out=h_sb[:], in_=h_0)
-        x_sb = keep.tile([P, IN], BF16, align_bytes=256)
+        x_sb = keep.tile([P, IN], BF16, align_bytes=512)
         nc.sync.dma_start(out=x_sb[:], in_=input_)
-        c_sb = keep.tile([P, H], BF16, align_bytes=256)
+        c_sb = keep.tile([P, H], BF16, align_bytes=512)
         nc.scalar.dma_start(out=c_sb[:], in_=c_0)
         nc.scalar.dma_start(out=bias_rows[0:1, :], in_=b_hh.unsqueeze(0))
 
@@ -111,7 +111,7 @@ def tile_qlstmcell_k_kernel(
             width = sum([block[2] for block in piece])
             first_byte = PACK * first_column(piece[0])
             n_bytes = PACK * width
-            tile = keep.tile([P, width], U32, align_bytes=256, name="w%d_%d" % (s, first_column(piece[0])))
+            tile = keep.tile([P, width], U32, align_bytes=512, name="w%d_%d" % (s, first_column(piece[0])))
             nc.sync.dma_start(
                 out=tile[:].bitcast(I32),
                 in_=words.rearrange("p n t -> p (n t)")[:, first_byte : first_byte + n_bytes].bitcast(I32),
@@ -218,13 +218,13 @@ def tile_qlstmcell_k_kernel(
         gate_values((G_BLOCK,))
         new = keep.tile([P, H], F32)
         combine(new, values[GATE_I], values[GATE_G], ALU.mult)
-        c_1 = keep.tile([P, H], F32, align_bytes=256)
+        c_1 = keep.tile([P, H], F32, align_bytes=512)
         combine(c_1, old, new, ALU.add)
         nc.sync.dma_start(out=out_1, in_=c_1[:])
         c_clipped = keep.tile([P, H], F32)
         clip(c_clipped, c_1, -1.0, 1.0)
 
-        h_1 = keep.tile([P, H], F32, align_bytes=256)
+        h_1 = keep.tile([P, H], F32, align_bytes=512)
         for block in (O_LEFT, O_RIGHT):
             start, width = block[1:]
             gate_values((block,))

@@ -86,16 +86,16 @@ def tile_qlstmcell_k_kernel(
         nc.sync.dma_start(out=h_sb[:], in_=h_0)
         x_sb = keep.tile([P, IN], BF16, align_bytes=512)
         nc.sync.dma_start(out=x_sb[:], in_=input_)
+        for quadrant in range(QUADRANTS):
+            rows = slice(ROWS * quadrant, ROWS * (quadrant + 1))
+            nc.sync.dma_start(
+                out=hh_planes[32 * quadrant : 32 * quadrant + 16, :].bitcast(I32),
+                in_=W_hh_scales[0, rows, :].rearrange("r (j n) -> j r n", j=PLANES).bitcast(I32),
+            )
         c_sb = keep.tile([P, H], BF16, align_bytes=512)
         nc.scalar.dma_start(out=c_sb[:], in_=c_0)
         nc.scalar.dma_start(out=bias_rows[0:1, :], in_=b_hh.unsqueeze(0))
 
-        for quadrant in range(QUADRANTS):
-            rows = slice(ROWS * quadrant, ROWS * (quadrant + 1))
-            nc.gpsimd.dma_start(
-                out=hh_planes[32 * quadrant : 32 * quadrant + 16, :].bitcast(F32),
-                in_=W_hh_scales[0, rows, :].rearrange("r (j n) -> j r n", j=PLANES).bitcast(F32),
-            )
         for tile_no in range(IH_PASSES // PLANES):
             for quadrant in range(QUADRANTS):
                 rows = slice(ROWS * quadrant, ROWS * (quadrant + 1))

from contextlib import ExitStack

import concourse.masks as masks
import concourse.mybir as mybir

F32 = mybir.dt.float32
BF16 = mybir.dt.bfloat16
I32 = mybir.dt.int32
U32 = mybir.dt.uint32
U8 = mybir.dt.uint8
FP8X4 = mybir.dt.float8_e4m3fn_x4
ALU = mybir.AluOpType

P = 128
PACK = 4
K_PASS = P * PACK
IN = 8192
H = 512
IH_PASSES = IN // K_PASS
PASSES = 1 + IH_PASSES
QUADRANTS = 4
ROWS = 4
PLANES = 4

GATE_F, GATE_I, GATE_O, GATE_G = 0, 1, 2, 3
HARD_SIGMOID = (1.0 / 6.0, 0.5, 0.0, 1.0)
HARD_TANH = (1.0, 0.0, -1.0, 1.0)
GATE_FUNCTION = {GATE_F: HARD_SIGMOID, GATE_I: HARD_SIGMOID, GATE_O: HARD_SIGMOID, GATE_G: HARD_TANH}

TAIL_PASSES = 7
SPLIT_PASSES = 3

F_BLOCK = (GATE_F, 0, H)
I_BLOCK = (GATE_I, 0, H)
G_BLOCK = (GATE_G, 0, H)
O_LEFT = (GATE_O, 0, H // 2)
O_RIGHT = (GATE_O, H // 2, H // 2)
BLOCKS = (F_BLOCK, I_BLOCK, O_LEFT, O_RIGHT, G_BLOCK)
HALVES = (slice(0, H // 2), slice(H // 2, H))

FLOPS = 2 * P * (IN + H) * 4 * H


def weight_stream():
    tail = range(PASSES - TAIL_PASSES, PASSES)
    stream = [(s, BLOCKS) for s in range(PASSES - TAIL_PASSES)]
    stream.extend([(s, (F_BLOCK, I_BLOCK)) for s in tail])
    stream.extend([(s, (G_BLOCK,)) for s in tail])
    stream.extend([(s, (O_LEFT, O_RIGHT)) for s in tail[:-SPLIT_PASSES]])
    stream.extend([(s, (O_LEFT,)) for s in tail[-SPLIT_PASSES:]])
    stream.extend([(s, (O_RIGHT,)) for s in tail[-SPLIT_PASSES:]])
    return stream


def first_column(block):
    return H * block[0] + block[1]


def tile_qlstmcell_k_kernel(
    tc, input_, h_0, c_0, W_ih_words, W_ih_scales, W_hh_words, W_hh_scales, b_hh, out_0, out_1
):
    nc = tc.nc
    with ExitStack() as ctx:
        keep = ctx.enter_context(tc.tile_pool(name="keep", bufs=1))
        stage = ctx.enter_context(tc.tile_pool(name="stage", bufs=3))
        acc_pool = ctx.enter_context(tc.psum_pool(name="acc", bufs=1))
        work_pool = ctx.enter_context(tc.psum_pool(name="work", bufs=3))
        ctx.enter_context(tc.manual_schedule())

        hh_planes = keep.tile([P, H], U8, align_bytes=512)
        nc.vector.memset(hh_planes[:].bitcast(I32), 0)
        ih_planes = []
        for tile_no in range(IH_PASSES // PLANES):
            planes = keep.tile([P, 4 * H], U8, align_bytes=512, name="ih_planes%d" % tile_no)
            nc.vector.memset(planes[:].bitcast(I32), 0)
            ih_planes.append(planes)

        identity = keep.tile([P, P], F32)
        masks.make_identity(nc, identity[:])
        bias_rows = keep.tile([P, 4 * H], BF16, align_bytes=512)
        nc.vector.memset(bias_rows[:].bitcast(I32), 0)
        ones = keep.tile([P, P], BF16)
        nc.vector.memset(ones[:], 1.0)

        h_sb = keep.tile([P, H], BF16, align_bytes=512)
        nc.sync.dma_start(out=h_sb[:], in_=h_0)
        x_sb = keep.tile([P, IN], BF16, align_bytes=512)
        nc.sync.dma_start(out=x_sb[:], in_=input_)
        for quadrant in range(QUADRANTS):
            rows = slice(ROWS * quadrant, ROWS * (quadrant + 1))
            nc.sync.dma_start(
                out=hh_planes[32 * quadrant : 32 * quadrant + 16, :].bitcast(I32),
                in_=W_hh_scales[0, rows, :].rearrange("r (j n) -> j r n", j=PLANES).bitcast(I32),
            )
        c_sb = keep.tile([P, H], BF16, align_bytes=512)
        nc.scalar.dma_start(out=c_sb[:], in_=c_0)
        nc.scalar.dma_start(out=bias_rows[0:1, :], in_=b_hh.unsqueeze(0))

        for tile_no in range(IH_PASSES // PLANES):
            for quadrant in range(QUADRANTS):
                rows = slice(ROWS * quadrant, ROWS * (quadrant + 1))
                nc.gpsimd.dma_start(
                    out=ih_planes[tile_no][32 * quadrant : 32 * quadrant + 16, :].bitcast(F32),
                    in_=W_ih_scales[PLANES * tile_no : PLANES * (tile_no + 1), rows, :].bitcast(F32),
                )

        stream = weight_stream()
        word_tiles = []
        for s, piece in stream:
            words = W_hh_words[0] if s == 0 else W_ih_words[s - 1]
            width = sum([block[2] for block in piece])
            first_byte = PACK * first_column(piece[0])
            n_bytes = PACK * width
            tile = keep.tile([P, width], U32, align_bytes=512, name="w%d_%d" % (s, first_column(piece[0])))
            nc.sync.dma_start(
                out=tile[:].bitcast(I32),
                in_=words.rearrange("p n t -> p (n t)")[:, first_byte : first_byte + n_bytes].bitcast(I32),
            )
            word_tiles.append(tile)

        x_codes = keep.tile([P, PASSES, P], U32, align_bytes=64)
        x_scales = keep.tile([P, PASSES, P], U8, align_bytes=64)

        def quantise_passes(words, first_pass, n_passes, copy_out):
            flipped = work_pool.tile([P, n_passes, 2, P], F32, tag="work")
            for s in range(n_passes):
                for u in range(2):
                    nc.tensor.transpose(
                        flipped[:, s, u, :], words[:, 256 * s + u : 256 * (s + 1) : 2], identity[:]
                    )
            grouped = stage.tile([P, n_passes, P, PACK], BF16, align_bytes=64, tag="grouped")
            copy_out(out=grouped[:].bitcast(F32), in_=flipped[:].rearrange("p s u b -> p s b u"))
            passes = slice(first_pass, first_pass + n_passes)
            nc.vector.quantize_mx(
                out=x_codes[:, passes, :].rearrange("p s b -> p (s b)").bitcast(FP8X4),
                scales=x_scales[:, passes, :].rearrange("p s b -> p (s b)"),
                in_=grouped[:].rearrange("p s b t -> p (s b t)"),
            )

        quantise_passes(h_sb[:].bitcast(F32), 0, 1, nc.vector.tensor_copy)
        x_words = x_sb[:].bitcast(F32)
        for pair in range(IH_PASSES // 2):
            quantise_passes(
                x_words[:, 512 * pair : 512 * (pair + 1)],
                1 + 2 * pair,
                2,
                nc.scalar.copy if pair % 2 == 0 else nc.vector.tensor_copy,
            )

        gate_bias = keep.tile([P, 4, H], F32)
        for gate in range(4):
            scale, shift = GATE_FUNCTION[gate][:2]
            spread = work_pool.tile([P, H], F32, tag="work")
            nc.tensor.matmul(
                out=spread[:], lhsT=ones[:], rhs=bias_rows[:, H * gate : H * (gate + 1)], start=True, stop=True
            )
            nc.vector.tensor_scalar(
                out=gate_bias[:, gate, :], in0=spread[:], scalar1=scale, scalar2=shift, op0=ALU.mult, op1=ALU.add
            )

        sums = {block: acc_pool.tile([P, block[2]], F32, name="sums%d" % first_column(block)) for block in BLOCKS}
        for (s, piece), tile in zip(stream, word_tiles):
            for block in piece:
                gate, start, width = block
                place = first_column(block) - first_column(piece[0])
                if s == 0:
                    plane = hh_planes[ROWS * gate : P, start : start + width]
                else:
                    group = s - 1
                    column = first_column(block)
                    plane = ih_planes[group // PLANES][ROWS * (group % PLANES) : P, column : column + width]
                nc.tensor.matmul_mx(
                    out=sums[block][:],
                    lhsT=x_codes[:, s, :].bitcast(FP8X4),
                    lhsT_scale=x_scales[:, s, :],
                    rhs=tile[:, place : place + width].bitcast(FP8X4),
                    rhs_scale=plane,
                    start=(s == 0),
                    stop=(s == PASSES - 1),
                )

        values = [keep.tile([P, H], F32, name="gate%d" % gate) for gate in range(4)]

        def halves(first, width):
            return (slice(first, first + width // 2), slice(first + width // 2, first + width))

        def gate_values(blocks):
            for block in blocks:
                gate, start, width = block
                for cols in halves(0, width):
                    in_gate = slice(start + cols.start, start + cols.stop)
                    nc.vector.scalar_tensor_tensor(
                        out=values[gate][:, in_gate],
                        in0=sums[block][:, cols],
                        scalar=GATE_FUNCTION[gate][0],
                        in1=gate_bias[:, gate, in_gate],
                        op0=ALU.mult,
                        op1=ALU.add,
                    )
            for gate, start, width in blocks:
                low, high = GATE_FUNCTION[gate][2:]
                clip(values[gate], values[gate], low, high, halves(start, width))

        def clip(out, in0, low, high, parts=HALVES):
            for cols in parts:
                nc.vector.tensor_scalar(
                    out=out[:, cols], in0=in0[:, cols], scalar1=low, scalar2=high, op0=ALU.max, op1=ALU.min
                )

        def combine(out, in0, in1, op, parts=HALVES):
            for cols in parts:
                nc.vector.tensor_tensor(out=out[:, cols], in0=in0[:, cols], in1=in1[:, cols], op=op)

        gate_values((F_BLOCK, I_BLOCK))
        old = keep.tile([P, H], F32)
        combine(old, values[GATE_F], c_sb, ALU.mult)

        gate_values((G_BLOCK,))
        new = keep.tile([P, H], F32)
        combine(new, values[GATE_I], values[GATE_G], ALU.mult)
        c_1 = keep.tile([P, H], F32, align_bytes=512)
        combine(c_1, old, new, ALU.add)
        nc.sync.dma_start(out=out_1, in_=c_1[:])
        c_clipped = keep.tile([P, H], F32)
        clip(c_clipped, c_1, -1.0, 1.0)

        h_1 = keep.tile([P, H], F32, align_bytes=512)
        for block in (O_LEFT, O_RIGHT):
            start, width = block[1:]
            gate_values((block,))
            combine(h_1, values[GATE_O], c_clipped, ALU.mult, halves(start, width))
            nc.sync.dma_start(out=out_0[:, start : start + width], in_=h_1[:, start : start + width])
